import numpy as np
import ml_dtypes


def mxq(x, axis, fmt="e4m3"):
    dtype, down = {"e4m3": (ml_dtypes.float8_e4m3fn, 7), "e5m2": (ml_dtypes.float8_e5m2, 14)}[fmt]
    v = np.moveaxis(np.asarray(x, np.float32).astype(ml_dtypes.bfloat16).astype(np.float64), axis, -1)
    blocks = v.reshape(v.shape[:-1] + (-1, 32))
    amax = np.abs(blocks).max(-1, keepdims=True)
    byte = np.maximum(np.where(amax > 0, np.frexp(amax)[1] - 1 + 127, 0) - down, 1)
    scale = np.exp2(byte - 127.0)
    codes = (blocks / scale).astype(np.float32).astype(dtype).astype(np.float64)
    return np.moveaxis((codes * scale).reshape(v.shape), -1, axis)


WIDE = False


def mx_kscale(k):
    if not WIDE:
        return np.ones(k)
    levels = np.array([10, -10, 5, -5, 0])
    if k % 512:
        return np.exp2(np.random.permutation(np.resize(levels, k // 32))).repeat(32)
    a = np.empty((k // 512, 16))
    for p in range(k // 512):
        a[p, :8] = np.random.permutation(np.resize(levels, 8))
        for g in range(8):
            far = levels[np.abs(levels - a[p, g]) >= 10]
            a[p, g + 8] = far[np.random.randint(len(far))]
    return np.exp2(a.ravel()).repeat(32)


BF16 = ml_dtypes.bfloat16


def bf(x):
    return np.asarray(x, np.float32).astype(BF16)


def f64(x):
    return np.asarray(x).astype(np.float64)


B, S, D, E, NS, C = 1, 1024, 512, 512, 256, 512


def softmax(z):
    e = np.exp(z - z.max(-1, keepdims=True))
    return e / e.sum(-1, keepdims=True)


def setup_inputs():
    s, t = mx_kscale(D), mx_kscale(E)
    return {"x": bf(np.random.standard_normal((B, S, D)) * s),
            "Wk": bf(np.random.standard_normal((D, E)) / np.sqrt(D) / s[:, None] * t),
            "bk": bf(np.random.standard_normal(E) * 0.2 * t),
            "Wq": bf(np.random.standard_normal((D, E)) / np.sqrt(D) / s[:, None] * t),
            "bq": bf(np.random.standard_normal(E) * 0.2 * t),
            "slot_keys": bf(np.random.standard_normal((NS, E)) / t),
            "scale": bf((2.0 + 0.2 * np.random.standard_normal(1)) / np.sqrt(E))}


def reference(x, Wk, bk, Wq, bq, slot_keys, scale):
    xq = mxq(f64(x), 2, "e4m3")
    sq = mxq(f64(slot_keys), 1, "e4m3")
    k = (xq @ mxq(f64(Wk), 0, "e4m3")) + f64(bk)
    q = (xq @ mxq(f64(Wq), 0, "e4m3")) + f64(bq)
    ww = softmax((mxq(k, 2, "e4m3") @ sq.T) * f64(scale))
    rw = softmax((mxq(q, 2, "e4m3") @ sq.T) * f64(scale))
    return ww, rw

@@ -1,0 +1,256 @@
+from contextlib import ExitStack
+
+import concourse.mybir as mybir
+from concourse.masks import make_identity
+
+F32 = mybir.dt.float32
+BF16 = mybir.dt.bfloat16
+U32 = mybir.dt.uint32
+U8 = mybir.dt.uint8
+FP8X4 = mybir.dt.float8_e4m3fn_x4
+ALU = mybir.AluOpType
+ACT = mybir.ActivationFunctionType
+AX = mybir.AxisListType
+
+S, D, E, NS = 1024, 512, 512, 256
+P = 128
+NT = S // P
+BANK = F32
+W_ON_SCALAR = [(1, 1)]
+NORM_BOTH_ON_VECTOR_FROM = 8
+
+FLOPS = 2 * (2 * S * D * E) + 2 * (2 * S * E * NS)
+
+
+def tile_slotmemoryphasor_pa_kernel(tc, x, Wk, bk, Wq, bq, slot_keys, scale, out_0, out_1):
+    nc = tc.nc
+    x_v = x.flatten_outer_dims().rearrange("(p i) d -> p i d", i=NT)
+    out_v = [o.flatten_outer_dims().rearrange("(p i) n -> p i n", i=NT) for o in (out_0, out_1)]
+    w_dram = (Wk, Wq)
+    b_dram = (bk, bq)
+
+    with ExitStack() as ctx:
+        const = ctx.enter_context(tc.tile_pool(name="const", bufs=1))
+        work = ctx.enter_context(tc.tile_pool(name="work", bufs=4))
+        psum = ctx.enter_context(tc.psum_pool(name="psum", bufs=2))
+
+        sc_bf = const.tile([P, 1], BF16, name="sc_bf")
+        b_stage = const.tile([1, 2, E], BF16, name="b_stage")
+        w_raw = [const.tile([P, 4, E], BF16, name="w_raw%d" % a) for a in range(2)]
+        x_sb = [const.tile([P, 2, D], BF16, name="x_sb%d" % j) for j in range(NT // 2)]
+        s_sb = const.tile([P, 2, E], BF16, name="s_sb")
+
+        def load_w(a):
+            nc.sync.dma_start(out=w_raw[a][:], in_=w_dram[a].rearrange("(p j) c -> p j c", j=4))
+
+        def load_x(j):
+            nc.sync.dma_start(out=x_sb[j][:], in_=x_v[:, 2 * j : 2 * j + 2, :])
+
+        nc.sync.dma_start(out=sc_bf[:], in_=scale.partition_broadcast(P))
+        for a in range(2):
+            nc.sync.dma_start(out=b_stage[0:1, a, :], in_=b_dram[a].unsqueeze(0))
+        load_w(0)
+        load_x(0)
+        load_w(1)
+        load_x(1)
+        nc.sync.dma_start(out=s_sb[:], in_=slot_keys.rearrange("(i p) e -> p i e", p=P))
+        load_x(2)
+        load_x(3)
+
+        warm = const.tile([P, 1], F32, name="warm")
+        warm2 = const.tile([P, 1], F32, name="warm2")
+        nc.vector.memset(warm[:], 0.0)
+        nc.scalar.activation(out=warm2[:], in_=warm[:], func=ACT.Exp)
+
+        b_row = const.tile([P, 2, E], BF16, name="b_row")
+        nc.vector.memset(b_row[:], 0.0)
+        ones = const.tile([P, P], BF16, name="ones")
+        nc.vector.memset(ones[:], 1.0)
+        ident = const.tile([P, P], F32, name="ident")
+        make_identity(nc, ident[:])
+        nc.vector.tensor_copy(out=b_row[0:1, :, :], in_=b_stage[0:1, :, :])
+
+        s32 = const.tile([P, 1], F32, name="s32")
+        sg0 = const.tile([P, 1], F32, name="sg0")
+        sgn = const.tile([P, 1], F32, name="sgn")
+        abs_s = const.tile([P, 1], F32, name="abs_s")
+        neg_s = const.tile([P, 1], F32, name="neg_s")
+        nc.vector.tensor_copy(out=s32[:], in_=sc_bf[:])
+        nc.vector.tensor_scalar(out=sg0[:], in0=s32[:], scalar1=0.0, scalar2=None, op0=ALU.is_ge)
+        nc.vector.tensor_scalar(out=sgn[:], in0=sg0[:], scalar1=2.0, scalar2=-1.0, op0=ALU.mult, op1=ALU.add)
+        nc.vector.tensor_tensor(out=abs_s[:], in0=s32[:], in1=sgn[:], op=ALU.mult)
+        nc.vector.tensor_scalar(out=neg_s[:], in0=abs_s[:], scalar1=-1.0, scalar2=None, op0=ALU.mult)
+
+        def turn_words(dst_bank, src_words, every_second):
+            for u in range(2):
+                if every_second:
+                    in_ = src_words[:, u : 2 * P : 2]
+                else:
+                    in_ = src_words[:, u * P : (u + 1) * P]
+                nc.tensor.transpose(out=dst_bank[:, u, :], in_=in_, identity=ident[:])
+
+        def quantize(codes, scales, grouped):
+            nc.vector.quantize_mx(
+                out=codes[:].bitcast(FP8X4),
+                scales=scales[:],
+                in_=grouped[:].rearrange("p i r t -> p (i r t)"),
+            )
+
+        w_grp = [const.tile([P, 4 * E], BF16, name="w_grp%d" % a, align_bytes=64) for a in range(2)]
+        w_cod = [const.tile([P, E], U32, name="w_cod%d" % a, align_bytes=64) for a in range(2)]
+        w_scl = [const.tile([P, E], U8, name="w_scl%d" % a, align_bytes=64) for a in range(2)]
+
+        def prep_w(a):
+            src = w_raw[a][:].rearrange("p j (m u e) -> p u m e j", u=2, e=2)
+            dst = w_grp[a][:].rearrange("p (u m e j) -> p u m e j", u=2, e=2, j=4)
+            for u in range(2):
+                if (a, u) in W_ON_SCALAR:
+                    nc.scalar.copy(out=dst[:, u], in_=src[:, u])
+                else:
+                    nc.vector.tensor_copy(out=dst[:, u], in_=src[:, u])
+
+        def quant_w(a):
+            for u in range(2):
+                cols = slice(u * E // 2, (u + 1) * E // 2)
+                nc.vector.quantize_mx(
+                    out=w_cod[a][:, cols].bitcast(FP8X4),
+                    scales=w_scl[a][:, cols],
+                    in_=w_grp[a][:, u * 2 * E : (u + 1) * 2 * E],
+                )
+
+        bias_bc = const.tile([P, 2, E], BF16, name="bias_bc")
+
+        def prep_bias(a):
+            pb = psum.tile([P, E], F32, name="pb", tag="s2", bufs=2)
+            nc.tensor.matmul(out=pb[:], lhsT=ones[:], rhs=b_row[:, a, :], start=True, stop=True)
+            nc.scalar.copy(
+                out=bias_bc[:, a, :].rearrange("p (u m e) -> p u m e", u=2, e=2),
+                in_=pb[:].rearrange("p (m u e) -> p u m e", u=2, e=2),
+            )
+
+        x_grp = [const.tile([P, 2, P, 4], BF16, name="x_grp%d" % j, align_bytes=64) for j in range(NT // 2)]
+        x_cod = [const.tile([P, 2 * P], U32, name="x_cod%d" % j, align_bytes=64) for j in range(NT // 2)]
+        x_scl = [const.tile([P, 2 * P], U8, name="x_scl%d" % j, align_bytes=64) for j in range(NT // 2)]
+        s_sg = const.tile([P, 2, E], BF16, name="s_sg")
+        s_grp = const.tile([P, 2, P, 4], BF16, name="s_grp", align_bytes=64)
+        s_cod = const.tile([P, NS], U32, name="s_cod", align_bytes=64)
+        s_scl = const.tile([P, NS], U8, name="s_scl", align_bytes=64)
+
+        def turn_rows(rows, grouped):
+            bank = psum.tile([P, 2, 2, P], F32, name="tp", tag="tp", bufs=3)
+            for i in range(2):
+                turn_words(bank[:, i], rows[:, i, :].bitcast(F32), True)
+            nc.scalar.copy(out=grouped[:].bitcast(F32), in_=bank[:].rearrange("p i u r -> p i r u"))
+
+        st = {}
+
+        def stage1(i):
+            kq_sb = work.tile([P, 2, E], BF16, name="kq_sb")
+            cols = slice((i % 2) * P, (i % 2 + 1) * P)
+            for a in range(2):
+                s1 = psum.tile([P, E], BANK, name="s1", tag="s1", bufs=3)
+                nc.tensor.matmul_mx(
+                    out=s1[:],
+                    lhsT=x_cod[i // 2][:, cols].bitcast(FP8X4),
+                    lhsT_scale=x_scl[i // 2][:, cols],
+                    rhs=w_cod[a][:].bitcast(FP8X4),
+                    rhs_scale=w_scl[a][:],
+                    start=True,
+                    stop=True,
+                )
+                nc.vector.tensor_tensor(out=kq_sb[:, a, :], in0=s1[:], in1=bias_bc[:, a, :], op=ALU.add)
+            st[("kq_sb", i)] = kq_sb
+
+        def turn_kq(i):
+            kq_sb = st[("kq_sb", i)]
+            kq_grp = work.tile([P, 2, P, 4], BF16, name="kq_grp", align_bytes=64)
+            bank = psum.tile([P, 2, 2, P], F32, name="tp2", tag="tp", bufs=3)
+            for a in range(2):
+                turn_words(bank[:, a], kq_sb[:, a, :].bitcast(F32), False)
+            nc.scalar.copy(out=kq_grp[:].bitcast(F32), in_=bank[:].rearrange("p a u r -> p a r u"))
+            st[("kq_grp", i)] = kq_grp
+
+        def quant_kq(i):
+            kq_cod = work.tile([P, 2 * P], U32, name="kq_cod", align_bytes=64)
+            kq_scl = work.tile([P, 2 * P], U8, name="kq_scl", align_bytes=64)
+            quantize(kq_cod, kq_scl, st[("kq_grp", i)])
+            st[("kq_cod", i)] = (kq_cod, kq_scl)
+
+        def stage2(i):
+            kq_cod, kq_scl = st[("kq_cod", i)]
+            s2 = psum.tile([P, 2, NS], F32, name="s2", tag="s2", bufs=2)
+            for a in range(2):
+                cols = slice(a * P, (a + 1) * P)
+                nc.tensor.matmul_mx(
+                    out=s2[:, a, :],
+                    lhsT=kq_cod[:, cols].bitcast(FP8X4),
+                    lhsT_scale=kq_scl[:, cols],
+                    rhs=s_cod[:].bitcast(FP8X4),
+                    rhs_scale=s_scl[:],
+                    start=True,
+                    stop=True,
+                )
+            mx = work.tile([P, 2], F32, name="mx")
+            nb = work.tile([P, 2], F32, name="nb")
+            nc.vector.tensor_reduce(out=mx[:], in_=s2[:], axis=AX.X, op=ALU.max)
+            nc.vector.tensor_scalar(out=nb[:], in0=mx[:], scalar1=neg_s[:, 0:1], scalar2=None, op0=ALU.mult)
+            st[("s2", i)] = (s2, nb)
+
+        def exps(i):
+            s2, nb = st[("s2", i)]
+            ex = work.tile([P, 2, NS], F32, name="ex")
+            sm = work.tile([P, 2], F32, name="sm")
+            rs = work.tile([P, 2], F32, name="rs")
+            for a in range(2):
+                nc.scalar.activation(
+                    out=ex[:, a, :],
+                    in_=s2[:, a, :],
+                    func=ACT.Exp,
+                    bias=nb[:, a : a + 1],
+                    scale=abs_s[:, 0:1],
+                    accum_out=sm[:, a : a + 1],
+                )
+            nc.vector.reciprocal(out=rs[:], in_=sm[:])
+            st[("ex", i)] = (ex, rs)
+
+        def finish(i):
+            ex, rs = st[("ex", i)]
+            ot = work.tile([P, 2, NS], F32, name="ot")
+            for a in range(2):
+                if a == 0 or i >= NORM_BOTH_ON_VECTOR_FROM:
+                    nc.vector.tensor_scalar(
+                        out=ot[:, a, :], in0=ex[:, a, :], scalar1=rs[:, a : a + 1], scalar2=None, op0=ALU.mult
+                    )
+                else:
+                    nc.scalar.activation(out=ot[:, a, :], in_=ex[:, a, :], func=ACT.Copy, scale=rs[:, a : a + 1])
+                nc.sync.dma_start(out=out_v[a][:, i, :], in_=ot[:, a, :])
+
+        prep_bias(0)
+        prep_bias(1)
+        prep_w(0)
+        turn_rows(x_sb[0], x_grp[0])
+        quant_w(0)
+        quantize(x_cod[0], x_scl[0], x_grp[0])
+        prep_w(1)
+        quant_w(1)
+        turn_rows(x_sb[1], x_grp[1])
+        quantize(x_cod[1], x_scl[1], x_grp[1])
+        nc.vector.tensor_scalar(out=s_sg[:], in0=s_sb[:], scalar1=sgn[:, 0:1], scalar2=None, op0=ALU.mult)
+        turn_rows(s_sg, s_grp)
+        quantize(s_cod, s_scl, s_grp)
+
+        for step in range(NT + 4):
+            if step % 2 == 0 and step // 2 + 2 < NT // 2:
+                j = step // 2 + 2
+                turn_rows(x_sb[j], x_grp[j])
+                quantize(x_cod[j], x_scl[j], x_grp[j])
+            if step < NT:
+                stage1(step)
+                turn_kq(step)
+            if 0 <= step - 1 < NT:
+                quant_kq(step - 1)
+                stage2(step - 1)
+            if 0 <= step - 2 < NT:
+                exps(step - 2)
+            if 0 <= step - 3 < NT:
+                finish(step - 3)

@@ -10,13 +10,12 @@ U8 = mybir.dt.uint8
 FP8X4 = mybir.dt.float8_e4m3fn_x4
 ALU = mybir.AluOpType
 ACT = mybir.ActivationFunctionType
-AX = mybir.AxisListType
 
 S, D, E, NS = 1024, 512, 512, 256
 P = 128
 NT = S // P
 BANK = F32
-W_ON_SCALAR = [(1, 1)]
+W_ON_SCALAR = []
 NORM_BOTH_ON_VECTOR_FROM = 8
 
 FLOPS = 2 * (2 * S * D * E) + 2 * (2 * S * E * NS)
@@ -70,16 +69,8 @@ def tile_slotmemoryphasor_pa_kernel(tc, x, Wk, bk, Wq, bq, slot_keys, scale, out
         make_identity(nc, ident[:])
         nc.vector.tensor_copy(out=b_row[0:1, :, :], in_=b_stage[0:1, :, :])
 
-        s32 = const.tile([P, 1], F32, name="s32")
-        sg0 = const.tile([P, 1], F32, name="sg0")
-        sgn = const.tile([P, 1], F32, name="sgn")
-        abs_s = const.tile([P, 1], F32, name="abs_s")
         neg_s = const.tile([P, 1], F32, name="neg_s")
-        nc.vector.tensor_copy(out=s32[:], in_=sc_bf[:])
-        nc.vector.tensor_scalar(out=sg0[:], in0=s32[:], scalar1=0.0, scalar2=None, op0=ALU.is_ge)
-        nc.vector.tensor_scalar(out=sgn[:], in0=sg0[:], scalar1=2.0, scalar2=-1.0, op0=ALU.mult, op1=ALU.add)
-        nc.vector.tensor_tensor(out=abs_s[:], in0=s32[:], in1=sgn[:], op=ALU.mult)
-        nc.vector.tensor_scalar(out=neg_s[:], in0=abs_s[:], scalar1=-1.0, scalar2=None, op0=ALU.mult)
+        nc.vector.tensor_scalar(out=neg_s[:], in0=sc_bf[:], scalar1=-1.0, scalar2=None, op0=ALU.mult)
 
         def turn_words(dst_bank, src_words, every_second):
             for u in range(2):
@@ -131,7 +122,6 @@ def tile_slotmemoryphasor_pa_kernel(tc, x, Wk, bk, Wq, bq, slot_keys, scale, out
         x_grp = [const.tile([P, 2, P, 4], BF16, name="x_grp%d" % j, align_bytes=64) for j in range(NT // 2)]
         x_cod = [const.tile([P, 2 * P], U32, name="x_cod%d" % j, align_bytes=64) for j in range(NT // 2)]
         x_scl = [const.tile([P, 2 * P], U8, name="x_scl%d" % j, align_bytes=64) for j in range(NT // 2)]
-        s_sg = const.tile([P, 2, E], BF16, name="s_sg")
         s_grp = const.tile([P, 2, P, 4], BF16, name="s_grp", align_bytes=64)
         s_cod = const.tile([P, NS], U32, name="s_cod", align_bytes=64)
         s_scl = const.tile([P, NS], U8, name="s_scl", align_bytes=64)
@@ -190,24 +180,32 @@ def tile_slotmemoryphasor_pa_kernel(tc, x, Wk, bk, Wq, bq, slot_keys, scale, out
                     start=True,
                     stop=True,
                 )
-            mx = work.tile([P, 2], F32, name="mx")
+            sc = work.tile([P, 2, NS], F32, name="sc")
             nb = work.tile([P, 2], F32, name="nb")
-            nc.vector.tensor_reduce(out=mx[:], in_=s2[:], axis=AX.X, op=ALU.max)
-            nc.vector.tensor_scalar(out=nb[:], in0=mx[:], scalar1=neg_s[:, 0:1], scalar2=None, op0=ALU.mult)
-            st[("s2", i)] = (s2, nb)
+            for a in range(2):
+                nc.vector.tensor_scalar(
+                    out=sc[:, a, :],
+                    in0=s2[:, a, :],
+                    scalar1=neg_s[:, 0:1],
+                    scalar2=None,
+                    op0=ALU.mult,
+                    op1=ALU.min,
+                    accum_out=nb[:, a : a + 1],
+                )
+            st[("s2", i)] = (sc, nb)
 
         def exps(i):
-            s2, nb = st[("s2", i)]
+            sc, nb = st[("s2", i)]
             ex = work.tile([P, 2, NS], F32, name="ex")
             sm = work.tile([P, 2], F32, name="sm")
             rs = work.tile([P, 2], F32, name="rs")
             for a in range(2):
                 nc.scalar.activation(
                     out=ex[:, a, :],
-                    in_=s2[:, a, :],
+                    in_=sc[:, a, :],
                     func=ACT.Exp,
                     bias=nb[:, a : a + 1],
-                    scale=abs_s[:, 0:1],
+                    scale=-1.0,
                     accum_out=sm[:, a : a + 1],
                 )
             nc.vector.reciprocal(out=rs[:], in_=sm[:])
@@ -235,8 +233,7 @@ def tile_slotmemoryphasor_pa_kernel(tc, x, Wk, bk, Wq, bq, slot_keys, scale, out
         quant_w(1)
         turn_rows(x_sb[1], x_grp[1])
         quantize(x_cod[1], x_scl[1], x_grp[1])
-        nc.vector.tensor_scalar(out=s_sg[:], in0=s_sb[:], scalar1=sgn[:, 0:1], scalar2=None, op0=ALU.mult)
-        turn_rows(s_sg, s_grp)
+        turn_rows(s_sb, s_grp)
         quantize(s_cod, s_scl, s_grp)
 
         for step in range(NT + 4):

from contextlib import ExitStack

import concourse.mybir as mybir
from concourse.masks import make_identity

F32 = mybir.dt.float32
BF16 = mybir.dt.bfloat16
U32 = mybir.dt.uint32
U8 = mybir.dt.uint8
FP8X4 = mybir.dt.float8_e4m3fn_x4
ALU = mybir.AluOpType
ACT = mybir.ActivationFunctionType

S, D, E, NS = 1024, 512, 512, 256
P = 128
NT = S // P
BANK = F32
W_ON_SCALAR = []
NORM_BOTH_ON_VECTOR_FROM = 8

FLOPS = 2 * (2 * S * D * E) + 2 * (2 * S * E * NS)


def tile_slotmemoryphasor_pa_kernel(tc, x, Wk, bk, Wq, bq, slot_keys, scale, out_0, out_1):
    nc = tc.nc
    x_v = x.flatten_outer_dims().rearrange("(p i) d -> p i d", i=NT)
    out_v = [o.flatten_outer_dims().rearrange("(p i) n -> p i n", i=NT) for o in (out_0, out_1)]
    w_dram = (Wk, Wq)
    b_dram = (bk, bq)

    with ExitStack() as ctx:
        const = ctx.enter_context(tc.tile_pool(name="const", bufs=1))
        work = ctx.enter_context(tc.tile_pool(name="work", bufs=4))
        psum = ctx.enter_context(tc.psum_pool(name="psum", bufs=2))

        sc_bf = const.tile([P, 1], BF16, name="sc_bf")
        b_stage = const.tile([1, 2, E], BF16, name="b_stage")
        w_raw = [const.tile([P, 4, E], BF16, name="w_raw%d" % a) for a in range(2)]
        x_sb = [const.tile([P, 2, D], BF16, name="x_sb%d" % j) for j in range(NT // 2)]
        s_sb = const.tile([P, 2, E], BF16, name="s_sb")

        def load_w(a):
            nc.sync.dma_start(out=w_raw[a][:], in_=w_dram[a].rearrange("(p j) c -> p j c", j=4))

        def load_x(j):
            nc.sync.dma_start(out=x_sb[j][:], in_=x_v[:, 2 * j : 2 * j + 2, :])

        nc.sync.dma_start(out=sc_bf[:], in_=scale.partition_broadcast(P))
        for a in range(2):
            nc.sync.dma_start(out=b_stage[0:1, a, :], in_=b_dram[a].unsqueeze(0))
        load_w(0)
        load_x(0)
        load_w(1)
        load_x(1)
        nc.sync.dma_start(out=s_sb[:], in_=slot_keys.rearrange("(i p) e -> p i e", p=P))
        load_x(2)
        load_x(3)

        warm = const.tile([P, 1], F32, name="warm")
        warm2 = const.tile([P, 1], F32, name="warm2")
        nc.vector.memset(warm[:], 0.0)
        nc.scalar.activation(out=warm2[:], in_=warm[:], func=ACT.Exp)

        b_row = const.tile([P, 2, E], BF16, name="b_row")
        nc.vector.memset(b_row[:], 0.0)
        ones = const.tile([P, P], BF16, name="ones")
        nc.vector.memset(ones[:], 1.0)
        ident = const.tile([P, P], F32, name="ident")
        make_identity(nc, ident[:])
        nc.vector.tensor_copy(out=b_row[0:1, :, :], in_=b_stage[0:1, :, :])

        neg_s = const.tile([P, 1], F32, name="neg_s")
        nc.vector.tensor_scalar(out=neg_s[:], in0=sc_bf[:], scalar1=-1.0, scalar2=None, op0=ALU.mult)

        def turn_words(dst_bank, src_words, every_second):
            for u in range(2):
                if every_second:
                    in_ = src_words[:, u : 2 * P : 2]
                else:
                    in_ = src_words[:, u * P : (u + 1) * P]
                nc.tensor.transpose(out=dst_bank[:, u, :], in_=in_, identity=ident[:])

        def quantize(codes, scales, grouped):
            nc.vector.quantize_mx(
                out=codes[:].bitcast(FP8X4),
                scales=scales[:],
                in_=grouped[:].rearrange("p i r t -> p (i r t)"),
            )

        w_grp = [const.tile([P, 4 * E], BF16, name="w_grp%d" % a, align_bytes=64) for a in range(2)]
        w_cod = [const.tile([P, E], U32, name="w_cod%d" % a, align_bytes=64) for a in range(2)]
        w_scl = [const.tile([P, E], U8, name="w_scl%d" % a, align_bytes=64) for a in range(2)]

        def prep_w(a):
            src = w_raw[a][:].rearrange("p j (m u e) -> p u m e j", u=2, e=2)
            dst = w_grp[a][:].rearrange("p (u m e j) -> p u m e j", u=2, e=2, j=4)
            for u in range(2):
                if (a, u) in W_ON_SCALAR:
                    nc.scalar.copy(out=dst[:, u], in_=src[:, u])
                else:
                    nc.vector.tensor_copy(out=dst[:, u], in_=src[:, u])

        def quant_w(a):
            for u in range(2):
                cols = slice(u * E // 2, (u + 1) * E // 2)
                nc.vector.quantize_mx(
                    out=w_cod[a][:, cols].bitcast(FP8X4),
                    scales=w_scl[a][:, cols],
                    in_=w_grp[a][:, u * 2 * E : (u + 1) * 2 * E],
                )

        bias_bc = const.tile([P, 2, E], BF16, name="bias_bc")

        def prep_bias(a):
            pb = psum.tile([P, E], F32, name="pb", tag="s2", bufs=2)
            nc.tensor.matmul(out=pb[:], lhsT=ones[:], rhs=b_row[:, a, :], start=True, stop=True)
            nc.scalar.copy(
                out=bias_bc[:, a, :].rearrange("p (u m e) -> p u m e", u=2, e=2),
                in_=pb[:].rearrange("p (m u e) -> p u m e", u=2, e=2),
            )

        x_grp = [const.tile([P, 2, P, 4], BF16, name="x_grp%d" % j, align_bytes=64) for j in range(NT // 2)]
        x_cod = [const.tile([P, 2 * P], U32, name="x_cod%d" % j, align_bytes=64) for j in range(NT // 2)]
        x_scl = [const.tile([P, 2 * P], U8, name="x_scl%d" % j, align_bytes=64) for j in range(NT // 2)]
        s_grp = const.tile([P, 2, P, 4], BF16, name="s_grp", align_bytes=64)
        s_cod = const.tile([P, NS], U32, name="s_cod", align_bytes=64)
        s_scl = const.tile([P, NS], U8, name="s_scl", align_bytes=64)

        def turn_rows(rows, grouped):
            bank = psum.tile([P, 2, 2, P], F32, name="tp", tag="tp", bufs=3)
            for i in range(2):
                turn_words(bank[:, i], rows[:, i, :].bitcast(F32), True)
            nc.scalar.copy(out=grouped[:].bitcast(F32), in_=bank[:].rearrange("p i u r -> p i r u"))

        st = {}

        def stage1(i):
            kq_sb = work.tile([P, 2, E], BF16, name="kq_sb")
            cols = slice((i % 2) * P, (i % 2 + 1) * P)
            for a in range(2):
                s1 = psum.tile([P, E], BANK, name="s1", tag="s1", bufs=3)
                nc.tensor.matmul_mx(
                    out=s1[:],
                    lhsT=x_cod[i // 2][:, cols].bitcast(FP8X4),
                    lhsT_scale=x_scl[i // 2][:, cols],
                    rhs=w_cod[a][:].bitcast(FP8X4),
                    rhs_scale=w_scl[a][:],
                    start=True,
                    stop=True,
                )
                nc.vector.tensor_tensor(out=kq_sb[:, a, :], in0=s1[:], in1=bias_bc[:, a, :], op=ALU.add)
            st[("kq_sb", i)] = kq_sb

        def turn_kq(i):
            kq_sb = st[("kq_sb", i)]
            kq_grp = work.tile([P, 2, P, 4], BF16, name="kq_grp", align_bytes=64)
            bank = psum.tile([P, 2, 2, P], F32, name="tp2", tag="tp", bufs=3)
            for a in range(2):
                turn_words(bank[:, a], kq_sb[:, a, :].bitcast(F32), False)
            nc.scalar.copy(out=kq_grp[:].bitcast(F32), in_=bank[:].rearrange("p a u r -> p a r u"))
            st[("kq_grp", i)] = kq_grp

        def quant_kq(i):
            kq_cod = work.tile([P, 2 * P], U32, name="kq_cod", align_bytes=64)
            kq_scl = work.tile([P, 2 * P], U8, name="kq_scl", align_bytes=64)
            quantize(kq_cod, kq_scl, st[("kq_grp", i)])
            st[("kq_cod", i)] = (kq_cod, kq_scl)

        def stage2(i):
            kq_cod, kq_scl = st[("kq_cod", i)]
            s2 = psum.tile([P, 2, NS], F32, name="s2", tag="s2", bufs=2)
            for a in range(2):
                cols = slice(a * P, (a + 1) * P)
                nc.tensor.matmul_mx(
                    out=s2[:, a, :],
                    lhsT=kq_cod[:, cols].bitcast(FP8X4),
                    lhsT_scale=kq_scl[:, cols],
                    rhs=s_cod[:].bitcast(FP8X4),
                    rhs_scale=s_scl[:],
                    start=True,
                    stop=True,
                )
            sc = work.tile([P, 2, NS], F32, name="sc")
            nb = work.tile([P, 2], F32, name="nb")
            for a in range(2):
                nc.vector.tensor_scalar(
                    out=sc[:, a, :],
                    in0=s2[:, a, :],
                    scalar1=neg_s[:, 0:1],
                    scalar2=None,
                    op0=ALU.mult,
                    op1=ALU.min,
                    accum_out=nb[:, a : a + 1],
                )
            st[("s2", i)] = (sc, nb)

        def exps(i):
            sc, nb = st[("s2", i)]
            ex = work.tile([P, 2, NS], F32, name="ex")
            sm = work.tile([P, 2], F32, name="sm")
            rs = work.tile([P, 2], F32, name="rs")
            for a in range(2):
                nc.scalar.activation(
                    out=ex[:, a, :],
                    in_=sc[:, a, :],
                    func=ACT.Exp,
                    bias=nb[:, a : a + 1],
                    scale=-1.0,
                    accum_out=sm[:, a : a + 1],
                )
            nc.vector.reciprocal(out=rs[:], in_=sm[:])
            st[("ex", i)] = (ex, rs)

        def finish(i):
            ex, rs = st[("ex", i)]
            ot = work.tile([P, 2, NS], F32, name="ot")
            for a in range(2):
                if a == 0 or i >= NORM_BOTH_ON_VECTOR_FROM:
                    nc.vector.tensor_scalar(
                        out=ot[:, a, :], in0=ex[:, a, :], scalar1=rs[:, a : a + 1], scalar2=None, op0=ALU.mult
                    )
                else:
                    nc.scalar.activation(out=ot[:, a, :], in_=ex[:, a, :], func=ACT.Copy, scale=rs[:, a : a + 1])
                nc.sync.dma_start(out=out_v[a][:, i, :], in_=ot[:, a, :])

        prep_bias(0)
        prep_bias(1)
        prep_w(0)
        turn_rows(x_sb[0], x_grp[0])
        quant_w(0)
        quantize(x_cod[0], x_scl[0], x_grp[0])
        prep_w(1)
        quant_w(1)
        turn_rows(x_sb[1], x_grp[1])
        quantize(x_cod[1], x_scl[1], x_grp[1])
        turn_rows(s_sb, s_grp)
        quantize(s_cod, s_scl, s_grp)

        for step in range(NT + 4):
            if step % 2 == 0 and step // 2 + 2 < NT // 2:
                j = step // 2 + 2
                turn_rows(x_sb[j], x_grp[j])
                quantize(x_cod[j], x_scl[j], x_grp[j])
            if step < NT:
                stage1(step)
                turn_kq(step)
            if 0 <= step - 1 < NT:
                quant_kq(step - 1)
                stage2(step - 1)
            if 0 <= step - 2 < NT:
                exps(step - 2)
            if 0 <= step - 3 < NT:
                finish(step - 3)
